import numpy as np
import ml_dtypes


def mxq(x, axis, fmt="e4m3"):
    dtype, down = {"e4m3": (ml_dtypes.float8_e4m3fn, 7), "e5m2": (ml_dtypes.float8_e5m2, 14)}[fmt]
    v = np.moveaxis(np.asarray(x, np.float32).astype(ml_dtypes.bfloat16).astype(np.float64), axis, -1)
    blocks = v.reshape(v.shape[:-1] + (-1, 32))
    amax = np.abs(blocks).max(-1, keepdims=True)
    byte = np.maximum(np.where(amax > 0, np.frexp(amax)[1] - 1 + 127, 0) - down, 1)
    scale = np.exp2(byte - 127.0)
    codes = (blocks / scale).astype(np.float32).astype(dtype).astype(np.float64)
    return np.moveaxis((codes * scale).reshape(v.shape), -1, axis)


WIDE = False


def mx_kscale(k):
    if not WIDE:
        return np.ones(k)
    levels = np.array([10, -10, 5, -5, 0])
    a = np.random.permutation(np.resize(levels, k // 512 * 4)).reshape(k // 512, 4)
    idx = np.arange(k)
    return np.exp2(a[idx // 512, idx % 128 // 32])


BF16 = ml_dtypes.bfloat16


def bf(x):
    return np.asarray(x, np.float32).astype(BF16)


def f64(x):
    return np.asarray(x).astype(np.float64)


E2M1 = np.array([0.0, 0.5, 1.0, 1.5, 2.0, 3.0, 4.0, 6.0, -0.0, -0.5, -1.0, -1.5, -2.0, -3.0, -4.0, -6.0])


def pack_weight(w, fmt):
    k, n = w.shape
    w = f64(bf(w)).reshape(k // 32, 32, n)
    amax = np.abs(w).max(1)
    if fmt == "e4m3":
        byte = np.frexp(amax)[1] - 1 + 127 - 7
    else:
        mant, ex = np.frexp(amax / 6.0)
        byte = np.where(mant > 0.5, ex, ex - 1) + 127
    byte = np.clip(np.where(amax > 0, byte, 1), 1, 254)
    scaled = (w * np.exp2(127.0 - byte)[:, None, :]).reshape(k, n).astype(np.float32)
    by_word = np.ascontiguousarray(scaled.reshape(k // 512, 128, 4, n).transpose(0, 1, 3, 2))
    if fmt == "e4m3":
        words = by_word.astype(ml_dtypes.float8_e4m3fn).view(np.uint8)
    else:
        c = by_word.astype(ml_dtypes.float4_e2m1fn).view(np.uint8) & 0xF
        words = c[..., 0::2] | (c[..., 1::2] << 4)
    return np.ascontiguousarray(words), np.ascontiguousarray(byte.astype(np.uint8).reshape(k // 512, 16, n))


def unpack_weight(words, scales, fmt):
    g, p, n, _ = words.shape
    if fmt == "e4m3":
        vals = np.ascontiguousarray(words).view(ml_dtypes.float8_e4m3fn).astype(np.float64)
    else:
        nib = np.empty((g, p, n, 4), np.uint8)
        nib[..., 0::2] = words & 0xF
        nib[..., 1::2] = words >> 4
        vals = E2M1[nib]
    vals = vals * np.repeat(np.exp2(scales.astype(np.float64) - 127.0), 8, axis=1)[..., None]
    return vals.transpose(0, 1, 3, 2).reshape(g * 512, n)


T, D, F1, F2 = 128, 2048, 4096, 2048
EPS = 1e-3
FMT = "e4m3"


def _layernorm(x, gamma, beta):
    mu = np.mean(x, axis=-1, keepdims=True)
    var = np.mean(np.square(x - mu), axis=-1, keepdims=True)
    rsigma = 1.0 / np.sqrt(var + EPS)
    return (x - mu) * rsigma * gamma + beta


def _gelu_tanh(x):
    c = 0.7978845608028654
    return 0.5 * x * (1.0 + np.tanh(c * (x + 0.044715 * x * x * x)))


def setup_inputs():
    s = mx_kscale(D)
    t = mx_kscale(F1)
    u = np.minimum(t, 1.0 / t) ** 2
    inputs = bf(np.random.standard_normal((T, D)) + 0.5)
    gamma = bf((1.0 + 0.1 * np.random.standard_normal(D)) * s)
    beta = bf(0.1 * np.random.standard_normal(D) * s)
    fc1_words, fc1_scales = pack_weight(np.random.standard_normal((D, F1)) / np.sqrt(D) / s[:, None] * u[None, :], FMT)
    fc1_bias = bf(0.1 * np.random.standard_normal(F1) * u)
    fc2_words, fc2_scales = pack_weight(np.random.standard_normal((F1, F2)) * 1.5 / np.sqrt(F1) / u[:, None], FMT)
    fc2_bias = bf(0.1 * np.random.standard_normal(F2))
    return {"inputs": inputs,
            "gamma": gamma,
            "beta": beta,
            "fc1_kernel_words": fc1_words,
            "fc1_kernel_scales": fc1_scales,
            "fc1_bias": fc1_bias,
            "fc2_kernel_words": fc2_words,
            "fc2_kernel_scales": fc2_scales,
            "fc2_bias": fc2_bias}


def reference(inputs, gamma, beta, fc1_kernel_words, fc1_kernel_scales, fc1_bias, fc2_kernel_words, fc2_kernel_scales, fc2_bias):
    ln_out = _layernorm(f64(inputs), f64(gamma), f64(beta))
    fc1_out = (mxq(ln_out, 1, "e4m3") @ unpack_weight(fc1_kernel_words, fc1_kernel_scales, FMT)) + f64(fc1_bias)
    gelu_out = _gelu_tanh(fc1_out)
    fc2_out = (mxq(gelu_out, 1, "e4m3") @ unpack_weight(fc2_kernel_words, fc2_kernel_scales, FMT)) + f64(fc2_bias)
    return fc2_out

@@ -1,0 +1,266 @@
+from contextlib import ExitStack
+
+import concourse.mybir as mybir
+from concourse.masks import make_identity
+
+F32 = mybir.dt.float32
+BF16 = mybir.dt.bfloat16
+I32 = mybir.dt.int32
+U32 = mybir.dt.uint32
+U8 = mybir.dt.uint8
+FP8X4 = mybir.dt.float8_e4m3fn_x4
+ALU = mybir.AluOpType
+ACT = mybir.ActivationFunctionType
+
+P = 128
+D = 2048
+F1 = 4096
+F2 = 2048
+EPS = 1e-3
+FLOPS = 2 * P * (D * F1 + F1 * F2)
+
+
+def tile_layernormmlp_w_kernel(
+    tc,
+    inputs,
+    gamma,
+    beta,
+    fc1_kernel_words,
+    fc1_kernel_scales,
+    fc1_bias,
+    fc2_kernel_words,
+    fc2_kernel_scales,
+    fc2_bias,
+    out,
+):
+    nc = tc.nc
+    with ExitStack() as ctx:
+        keep = ctx.enter_context(tc.tile_pool(name="keep", bufs=1))
+        work = ctx.enter_context(tc.tile_pool(name="work", bufs=4))
+        psum = ctx.enter_context(tc.psum_pool(name="psum", bufs=4))
+        ctx.enter_context(tc.manual_schedule())
+
+        vec_rows = keep.tile([P, 512], BF16)
+        nc.vector.memset(vec_rows[:].bitcast(I32), 0)
+        planes1 = keep.tile([P, F1], U8, align_bytes=64)
+        nc.vector.memset(planes1[:].bitcast(I32), 0)
+        planes2 = keep.tile([P, 2, F2], U8, align_bytes=64)
+        nc.vector.memset(planes2[:].bitcast(I32), 0)
+        ident_bf = keep.tile([P, P], BF16)
+        make_identity(nc, ident_bf[:])
+        ident_f = keep.tile([P, P], F32)
+        make_identity(nc, ident_f[:])
+
+        x_sb = keep.tile([P, D], BF16)
+        nc.sync.dma_start(out=x_sb[:], in_=inputs)
+        nc.scalar.dma_start(out=vec_rows[0:4, :], in_=gamma.rearrange("(c n) -> c n", n=512))
+        nc.scalar.dma_start(out=vec_rows[4:8, :], in_=beta.rearrange("(c n) -> c n", n=512))
+        nc.scalar.dma_start(out=vec_rows[8:16, :], in_=fc1_bias.rearrange("(c n) -> c n", n=512))
+        nc.scalar.dma_start(out=vec_rows[16:20, :], in_=fc2_bias.rearrange("(c n) -> c n", n=512))
+        for q in range(4):
+            nc.sync.dma_start(
+                out=planes1[32 * q : 32 * q + 16, :].bitcast(I32),
+                in_=fc1_kernel_scales[:, 4 * q : 4 * q + 4, :].bitcast(I32),
+            )
+        for a in range(2):
+            for q in range(4):
+                nc.sync.dma_start(
+                    out=planes2[32 * q : 32 * q + 16, a, :].bitcast(I32),
+                    in_=fc2_kernel_scales[4 * a : 4 * a + 4, 4 * q : 4 * q + 4, :].bitcast(I32),
+                )
+        w1_view = fc1_kernel_words.rearrange("g p n t -> p g (n t)")
+        w1 = []
+        for c in range(4):
+            w1_c = keep.tile([P, 4, 1024], U32, name="w1_%d" % c, align_bytes=64)
+            nc.sync.dma_start(
+                out=w1_c[:].bitcast(I32),
+                in_=w1_view[:, :, 4096 * c : 4096 * (c + 1)].bitcast(I32),
+            )
+            w1.append(w1_c)
+        w2_view = fc2_kernel_words.rearrange("g p n t -> g p (n t)")
+        w2 = []
+        for g in range(7):
+            w2_g = keep.tile([P, F2], U32, name="w2_%d" % g, align_bytes=64)
+            nc.sync.dma_start(out=w2_g[:].bitcast(I32), in_=w2_view[g].bitcast(I32))
+            w2.append(w2_g)
+        w2_last = []
+        for j in range(4):
+            w2_l = keep.tile([P, 512], U32, name="w2_last_%d" % j, align_bytes=64)
+            nc.sync.dma_start(
+                out=w2_l[:].bitcast(I32),
+                in_=w2_view[7][:, 2048 * j : 2048 * (j + 1)].bitcast(I32),
+            )
+            w2_last.append(w2_l)
+
+        def spread(row, bank, half):
+            nc.tensor.matmul(
+                out=bank[:, 512 * half : 512 * (half + 1)],
+                lhsT=ident_bf[:, row : row + 1].to_broadcast([P, P]),
+                rhs=vec_rows[:],
+                start=True,
+                stop=True,
+            )
+
+        stats = keep.tile([P, 4, 6], F32)
+        for i in range(4):
+            nc.vector.bn_stats(out=stats[:, i, :], in_=x_sb[:, 512 * i : 512 * (i + 1)])
+        mean_var = keep.tile([P, 2], F32)
+        nc.vector.bn_aggr(out=mean_var[:], in_=stats[:].rearrange("p a b -> p (a b)"))
+        var_eps = keep.tile([P, 1], F32)
+        nc.vector.tensor_scalar(
+            out=var_eps[:], in0=mean_var[:, 1:2], scalar1=EPS, scalar2=None, op0=ALU.add
+        )
+        std = keep.tile([P, 1], F32)
+        nc.scalar.activation(out=std[:], in_=var_eps[:], func=ACT.Sqrt)
+
+        gam = []
+        bet = []
+        for i in range(2):
+            gam_i = psum.tile([P, 1024], BF16, tag="rot", name="gam_%d" % i)
+            spread(2 * i, gam_i, 0)
+            spread(2 * i + 1, gam_i, 1)
+            gam.append(gam_i)
+        for i in range(2):
+            bet_i = psum.tile([P, 1024], BF16, tag="rot", name="bet_%d" % i)
+            spread(4 + 2 * i, bet_i, 0)
+            spread(4 + 2 * i + 1, bet_i, 1)
+            bet.append(bet_i)
+
+        centred = keep.tile([P, D], F32)
+        for i in range(2):
+            cols = slice(1024 * i, 1024 * (i + 1))
+            nc.vector.scalar_tensor_tensor(
+                out=centred[:, cols],
+                in0=x_sb[:, cols],
+                scalar=mean_var[:, 0:1],
+                in1=gam[i][:],
+                op0=ALU.subtract,
+                op1=ALU.mult,
+            )
+        rstd = keep.tile([P, 1], F32)
+        nc.vector.reciprocal(out=rstd[:], in_=std[:])
+        ln_sorted = keep.tile([P, 4, 4, P], F32)
+        for g in range(4):
+            nc.vector.scalar_tensor_tensor(
+                out=ln_sorted[:, g],
+                in0=centred[:, 512 * g : 512 * (g + 1)].rearrange("q (p t) -> q t p", t=4),
+                scalar=rstd[:, 0:1],
+                in1=bet[g // 2][:, 512 * (g % 2) : 512 * (g % 2 + 1)].rearrange(
+                    "q (p t) -> q t p", t=4
+                ),
+                op0=ALU.mult,
+                op1=ALU.add,
+            )
+
+        b1_sorted = []
+        for i in range(4):
+            bank = psum.tile([P, 1024], BF16, tag="fix", name="b1_bank_%d" % i)
+            spread(8 + 2 * i, bank, 0)
+            spread(8 + 2 * i + 1, bank, 1)
+            b1_i = keep.tile([P, 2, 4, P], BF16, name="b1_sorted_%d" % i)
+            nc.scalar.copy(out=b1_i[:], in_=bank[:].rearrange("q (j p t) -> q j t p", j=2, t=4))
+            b1_sorted.append(b1_i)
+        b2_all = keep.tile([P, F2], BF16)
+        for i in range(2):
+            bank = psum.tile([P, 1024], BF16, tag="fix", name="b2_bank_%d" % i)
+            spread(16 + 2 * i, bank, 0)
+            spread(16 + 2 * i + 1, bank, 1)
+            nc.scalar.copy(out=b2_all[:, 1024 * i : 1024 * (i + 1)], in_=bank[:])
+
+        ln_grouped = keep.tile([P, 4, P, 4], BF16, align_bytes=64)
+        for g in range(4):
+            ln_t = psum.tile([P, 4, P], F32, tag="rot", name="ln_t_%d" % g)
+            for t in range(4):
+                nc.tensor.transpose(ln_t[:, t, :], ln_sorted[:, g, t, :], ident_f[:])
+            if g % 2 == 0:
+                nc.scalar.copy(out=ln_grouped[:, g], in_=ln_t[:].rearrange("p t r -> p r t"))
+            else:
+                nc.vector.tensor_copy(out=ln_grouped[:, g], in_=ln_t[:].rearrange("p t r -> p r t"))
+        ln_words = keep.tile([P, 4, P], U32, align_bytes=64)
+        ln_plane = keep.tile([P, 4, P], U8, align_bytes=64)
+        nc.vector.quantize_mx(
+            out=ln_words[:].rearrange("p g m -> p (g m)").bitcast(FP8X4),
+            scales=ln_plane[:].rearrange("p g m -> p (g m)"),
+            in_=ln_grouped[:].rearrange("p g r t -> p (g r t)"),
+        )
+
+        h_pre = {}
+        h_words = []
+        h_plane = []
+
+        def fc1(c):
+            for jj in range(2):
+                j = 2 * c + jj
+                acc = psum.tile([P, 512], F32, tag="rot", name="acc1_%d" % j)
+                for g in range(4):
+                    nc.tensor.matmul_mx(
+                        out=acc[:],
+                        lhsT=ln_words[:, g, :].bitcast(FP8X4),
+                        lhsT_scale=ln_plane[:, g, :],
+                        rhs=w1[c][:, g, 512 * jj : 512 * (jj + 1)].bitcast(FP8X4),
+                        rhs_scale=planes1[4 * g : P, 512 * j : 512 * (j + 1)],
+                        start=(g == 0),
+                        stop=(g == 3),
+                    )
+                pre = work.tile([P, 4, P], F32, tag="h_pre", name="h_pre_%d" % j)
+                nc.vector.tensor_tensor(
+                    out=pre[:],
+                    in0=acc[:].rearrange("q (p t) -> q t p", t=4),
+                    in1=b1_sorted[c][:, jj],
+                    op=ALU.add,
+                )
+                h_pre[j] = pre
+
+        def finish_h(c):
+            grouped = work.tile([P, 2, P, 4], BF16, tag="h_grouped", name="h_grouped_%d" % c, align_bytes=64)
+            for jj in range(2):
+                j = 2 * c + jj
+                h_t = psum.tile([P, 4, P], F32, tag="rot", name="h_t_%d" % j)
+                for t in range(4):
+                    nc.tensor.transpose(h_t[:, t, :], h_pre[j][:, t, :], ident_f[:])
+                nc.scalar.activation(
+                    out=grouped[:, jj],
+                    in_=h_t[:].rearrange("p t r -> p r t"),
+                    func=ACT.Gelu_apprx_tanh,
+                )
+            words = keep.tile([P, 2, P], U32, name="h_words_%d" % c, align_bytes=64)
+            plane = keep.tile([P, 2, P], U8, name="h_plane_%d" % c, align_bytes=64)
+            nc.vector.quantize_mx(
+                out=words[:].rearrange("p j m -> p (j m)").bitcast(FP8X4),
+                scales=plane[:].rearrange("p j m -> p (j m)"),
+                in_=grouped[:].rearrange("p j r t -> p (j r t)"),
+            )
+            h_words.append(words)
+            h_plane.append(plane)
+
+        fc1(0)
+        for c in range(1, 4):
+            fc1(c)
+            finish_h(c - 1)
+        finish_h(3)
+
+        acc2 = []
+        for j in range(4):
+            acc2_j = psum.tile([P, 512], F32, tag="fix", name="acc2_%d" % j)
+            acc2.append(acc2_j)
+        for g in range(8):
+            for j in range(4):
+                if g < 7:
+                    rhs = w2[g][:, 512 * j : 512 * (j + 1)]
+                else:
+                    rhs = w2_last[j][:]
+                nc.tensor.matmul_mx(
+                    out=acc2[j][:],
+                    lhsT=h_words[g // 2][:, g % 2, :].bitcast(FP8X4),
+                    lhsT_scale=h_plane[g // 2][:, g % 2, :],
+                    rhs=rhs.bitcast(FP8X4),
+                    rhs_scale=planes2[4 * (g % 4) : P, g // 4, 512 * j : 512 * (j + 1)],
+                    start=(g == 0),
+                    stop=(g == 7),
+                )
+        for j in range(4):
+            o_j = keep.tile([P, 512], F32, name="o_%d" % j)
+            nc.vector.tensor_tensor(
+                out=o_j[:], in0=acc2[j][:], in1=b2_all[:, 512 * j : 512 * (j + 1)], op=ALU.add
+            )
+            nc.sync.dma_start(out=out[:, 512 * j : 512 * (j + 1)], in_=o_j[:])

@@ -48,8 +48,6 @@ def tile_layernormmlp_w_kernel(
         nc.vector.memset(planes2[:].bitcast(I32), 0)
         ident_bf = keep.tile([P, P], BF16)
         make_identity(nc, ident_bf[:])
-        ident_f = keep.tile([P, P], F32)
-        make_identity(nc, ident_f[:])
 
         x_sb = keep.tile([P, D], BF16)
         nc.sync.dma_start(out=x_sb[:], in_=inputs)
@@ -58,15 +56,17 @@ def tile_layernormmlp_w_kernel(
         nc.scalar.dma_start(out=vec_rows[8:16, :], in_=fc1_bias.rearrange("(c n) -> c n", n=512))
         nc.scalar.dma_start(out=vec_rows[16:20, :], in_=fc2_bias.rearrange("(c n) -> c n", n=512))
         for q in range(4):
-            nc.sync.dma_start(
-                out=planes1[32 * q : 32 * q + 16, :].bitcast(I32),
-                in_=fc1_kernel_scales[:, 4 * q : 4 * q + 4, :].bitcast(I32),
+            nc.gpsimd.dma_start(
+                out=planes1[32 * q : 32 * q + 16, :].bitcast(F32),
+                in_=fc1_kernel_scales[:, 4 * q : 4 * q + 4, :].bitcast(F32),
             )
+        ident_f = keep.tile([P, P], F32)
+        make_identity(nc, ident_f[:])
         for a in range(2):
             for q in range(4):
-                nc.sync.dma_start(
-                    out=planes2[32 * q : 32 * q + 16, a, :].bitcast(I32),
-                    in_=fc2_kernel_scales[4 * a : 4 * a + 4, 4 * q : 4 * q + 4, :].bitcast(I32),
+                nc.gpsimd.dma_start(
+                    out=planes2[32 * q : 32 * q + 16, a, :].bitcast(F32),
+                    in_=fc2_kernel_scales[4 * a : 4 * a + 4, 4 * q : 4 * q + 4, :].bitcast(F32),
                 )
         w1_view = fc1_kernel_words.rearrange("g p n t -> p g (n t)")
         w1 = []

@@ -37,8 +37,11 @@ def tile_layernormmlp_w_kernel(
     with ExitStack() as ctx:
         keep = ctx.enter_context(tc.tile_pool(name="keep", bufs=1))
         work = ctx.enter_context(tc.tile_pool(name="work", bufs=4))
-        psum = ctx.enter_context(tc.psum_pool(name="psum", bufs=4))
+        psum = ctx.enter_context(tc.psum_pool(name="psum", bufs=1))
         ctx.enter_context(tc.manual_schedule())
+
+        def bank(i, shape, dtype, name):
+            return psum.tile(shape, dtype, tag="bank%d" % i, name=name)
 
         vec_rows = keep.tile([P, 512], BF16)
         nc.vector.memset(vec_rows[:].bitcast(I32), 0)
@@ -48,13 +51,17 @@ def tile_layernormmlp_w_kernel(
         nc.vector.memset(planes2[:].bitcast(I32), 0)
         ident_bf = keep.tile([P, P], BF16)
         make_identity(nc, ident_bf[:])
+        table = keep.tile([P, 1], F32)
+        nc.vector.memset(table[:], 1.0)
+        table_out = keep.tile([P, 2], F32)
+        nc.scalar.activation(out=table_out[:, 0:1], in_=table[:], func=ACT.Sqrt)
 
         x_sb = keep.tile([P, D], BF16)
         nc.sync.dma_start(out=x_sb[:], in_=inputs)
-        nc.scalar.dma_start(out=vec_rows[0:4, :], in_=gamma.rearrange("(c n) -> c n", n=512))
-        nc.scalar.dma_start(out=vec_rows[4:8, :], in_=beta.rearrange("(c n) -> c n", n=512))
-        nc.scalar.dma_start(out=vec_rows[8:16, :], in_=fc1_bias.rearrange("(c n) -> c n", n=512))
-        nc.scalar.dma_start(out=vec_rows[16:20, :], in_=fc2_bias.rearrange("(c n) -> c n", n=512))
+        nc.sync.dma_start(out=vec_rows[0:4, :], in_=gamma.rearrange("(c n) -> c n", n=512))
+        nc.sync.dma_start(out=vec_rows[4:8, :], in_=beta.rearrange("(c n) -> c n", n=512))
+        nc.sync.dma_start(out=vec_rows[8:16, :], in_=fc1_bias.rearrange("(c n) -> c n", n=512))
+        nc.sync.dma_start(out=vec_rows[16:20, :], in_=fc2_bias.rearrange("(c n) -> c n", n=512))
         for q in range(4):
             nc.gpsimd.dma_start(
                 out=planes1[32 * q : 32 * q + 16, :].bitcast(F32),
@@ -68,15 +75,19 @@ def tile_layernormmlp_w_kernel(
                     out=planes2[32 * q : 32 * q + 16, a, :].bitcast(F32),
                     in_=fc2_kernel_scales[4 * a : 4 * a + 4, 4 * q : 4 * q + 4, :].bitcast(F32),
                 )
-        w1_view = fc1_kernel_words.rearrange("g p n t -> p g (n t)")
+        w1_view = fc1_kernel_words.rearrange("g p n t -> g p (n t)")
         w1 = []
-        for c in range(4):
-            w1_c = keep.tile([P, 4, 1024], U32, name="w1_%d" % c, align_bytes=64)
+        for g in range(3):
+            w1_g = keep.tile([P, F1], U32, name="w1_%d" % g, align_bytes=64)
+            nc.sync.dma_start(out=w1_g[:].bitcast(I32), in_=w1_view[g].bitcast(I32))
+            w1.append(w1_g)
+        w1_last = []
+        for i in range(2):
+            w1_l = keep.tile([P, F1 // 2], U32, name="w1_last_%d" % i, align_bytes=64)
             nc.sync.dma_start(
-                out=w1_c[:].bitcast(I32),
-                in_=w1_view[:, :, 4096 * c : 4096 * (c + 1)].bitcast(I32),
+                out=w1_l[:].bitcast(I32), in_=w1_view[3][:, 8192 * i : 8192 * (i + 1)].bitcast(I32)
             )
-            w1.append(w1_c)
+            w1_last.append(w1_l)
         w2_view = fc2_kernel_words.rearrange("g p n t -> g p (n t)")
         w2 = []
         for g in range(7):
@@ -92,14 +103,41 @@ def tile_layernormmlp_w_kernel(
             )
             w2_last.append(w2_l)
 
-        def spread(row, bank, half):
+        def spread(row, dest, half):
             nc.tensor.matmul(
-                out=bank[:, 512 * half : 512 * (half + 1)],
+                out=dest[:, 512 * half : 512 * (half + 1)],
                 lhsT=ident_bf[:, row : row + 1].to_broadcast([P, P]),
                 rhs=vec_rows[:],
                 start=True,
                 stop=True,
             )
+
+        b2_all = keep.tile([P, F2], BF16)
+        for i in range(2):
+            b2_i = bank(4 + i, [P, 1024], BF16, "b2_bank_%d" % i)
+            spread(16 + 2 * i, b2_i, 0)
+            spread(16 + 2 * i + 1, b2_i, 1)
+            nc.scalar.copy(out=b2_all[:, 1024 * i : 1024 * (i + 1)], in_=b2_i[:])
+        gam = []
+        bet = []
+        for i in range(2):
+            gam_i = bank(i, [P, 1024], BF16, "gam_%d" % i)
+            spread(2 * i, gam_i, 0)
+            spread(2 * i + 1, gam_i, 1)
+            gam.append(gam_i)
+        for i in range(2):
+            bet_i = bank(2 + i, [P, 1024], BF16, "bet_%d" % i)
+            spread(4 + 2 * i, bet_i, 0)
+            spread(4 + 2 * i + 1, bet_i, 1)
+            bet.append(bet_i)
+        b1_sorted = []
+        for i in range(4):
+            b1_bank = bank((6, 7, 4, 5)[i], [P, 1024], BF16, "b1_bank_%d" % i)
+            spread(8 + 2 * i, b1_bank, 0)
+            spread(8 + 2 * i + 1, b1_bank, 1)
+            b1_i = keep.tile([P, 2, 4, P], BF16, name="b1_sorted_%d" % i)
+            nc.scalar.copy(out=b1_i[:], in_=b1_bank[:].rearrange("q (j p t) -> q j t p", j=2, t=4))
+            b1_sorted.append(b1_i)
 
         stats = keep.tile([P, 4, 6], F32)
         for i in range(4):
@@ -112,19 +150,6 @@ def tile_layernormmlp_w_kernel(
         )
         std = keep.tile([P, 1], F32)
         nc.scalar.activation(out=std[:], in_=var_eps[:], func=ACT.Sqrt)
-
-        gam = []
-        bet = []
-        for i in range(2):
-            gam_i = psum.tile([P, 1024], BF16, tag="rot", name="gam_%d" % i)
-            spread(2 * i, gam_i, 0)
-            spread(2 * i + 1, gam_i, 1)
-            gam.append(gam_i)
-        for i in range(2):
-            bet_i = psum.tile([P, 1024], BF16, tag="rot", name="bet_%d" % i)
-            spread(4 + 2 * i, bet_i, 0)
-            spread(4 + 2 * i + 1, bet_i, 1)
-            bet.append(bet_i)
 
         centred = keep.tile([P, D], F32)
         for i in range(2):
@@ -152,24 +177,9 @@ def tile_layernormmlp_w_kernel(
                 op1=ALU.add,
             )
 
-        b1_sorted = []
-        for i in range(4):
-            bank = psum.tile([P, 1024], BF16, tag="fix", name="b1_bank_%d" % i)
-            spread(8 + 2 * i, bank, 0)
-            spread(8 + 2 * i + 1, bank, 1)
-            b1_i = keep.tile([P, 2, 4, P], BF16, name="b1_sorted_%d" % i)
-            nc.scalar.copy(out=b1_i[:], in_=bank[:].rearrange("q (j p t) -> q j t p", j=2, t=4))
-            b1_sorted.append(b1_i)
-        b2_all = keep.tile([P, F2], BF16)
-        for i in range(2):
-            bank = psum.tile([P, 1024], BF16, tag="fix", name="b2_bank_%d" % i)
-            spread(16 + 2 * i, bank, 0)
-            spread(16 + 2 * i + 1, bank, 1)
-            nc.scalar.copy(out=b2_all[:, 1024 * i : 1024 * (i + 1)], in_=bank[:])
-
         ln_grouped = keep.tile([P, 4, P, 4], BF16, align_bytes=64)
         for g in range(4):
-            ln_t = psum.tile([P, 4, P], F32, tag="rot", name="ln_t_%d" % g)
+            ln_t = bank(g, [P, 4, P], F32, "ln_t_%d" % g)
             for t in range(4):
                 nc.tensor.transpose(ln_t[:, t, :], ln_sorted[:, g, t, :], ident_f[:])
             if g % 2 == 0:
@@ -183,39 +193,46 @@ def tile_layernormmlp_w_kernel(
             scales=ln_plane[:].rearrange("p g m -> p (g m)"),
             in_=ln_grouped[:].rearrange("p g r t -> p (g r t)"),
         )
+        nc.scalar.activation(out=table_out[:, 1:2], in_=table[:], func=ACT.Gelu_apprx_tanh)
 
-        h_pre = {}
         h_words = []
         h_plane = []
 
-        def fc1(c):
-            for jj in range(2):
-                j = 2 * c + jj
-                acc = psum.tile([P, 512], F32, tag="rot", name="acc1_%d" % j)
-                for g in range(4):
-                    nc.tensor.matmul_mx(
-                        out=acc[:],
-                        lhsT=ln_words[:, g, :].bitcast(FP8X4),
-                        lhsT_scale=ln_plane[:, g, :],
-                        rhs=w1[c][:, g, 512 * jj : 512 * (jj + 1)].bitcast(FP8X4),
-                        rhs_scale=planes1[4 * g : P, 512 * j : 512 * (j + 1)],
-                        start=(g == 0),
-                        stop=(g == 3),
-                    )
-                pre = work.tile([P, 4, P], F32, tag="h_pre", name="h_pre_%d" % j)
-                nc.vector.tensor_tensor(
-                    out=pre[:],
-                    in0=acc[:].rearrange("q (p t) -> q t p", t=4),
-                    in1=b1_sorted[c][:, jj],
-                    op=ALU.add,
+        acc1 = []
+        for j in range(8):
+            acc1_j = bank(j, [P, 512], F32, "acc1_%d" % j)
+            acc1.append(acc1_j)
+        for g in range(4):
+            for j in range(8):
+                if g < 3:
+                    rhs = w1[g][:, 512 * j : 512 * (j + 1)]
+                else:
+                    rhs = w1_last[j // 4][:, 512 * (j % 4) : 512 * (j % 4 + 1)]
+                nc.tensor.matmul_mx(
+                    out=acc1[j][:],
+                    lhsT=ln_words[:, g, :].bitcast(FP8X4),
+                    lhsT_scale=ln_plane[:, g, :],
+                    rhs=rhs.bitcast(FP8X4),
+                    rhs_scale=planes1[4 * g : P, 512 * j : 512 * (j + 1)],
+                    start=(g == 0),
+                    stop=(g == 3),
                 )
-                h_pre[j] = pre
+        h_pre = []
+        for j in range(8):
+            pre = keep.tile([P, 4, P], F32, name="h_pre_%d" % j)
+            nc.vector.tensor_tensor(
+                out=pre[:],
+                in0=acc1[j][:].rearrange("q (p t) -> q t p", t=4),
+                in1=b1_sorted[j // 2][:, j % 2],
+                op=ALU.add,
+            )
+            h_pre.append(pre)
 
         def finish_h(c):
             grouped = work.tile([P, 2, P, 4], BF16, tag="h_grouped", name="h_grouped_%d" % c, align_bytes=64)
             for jj in range(2):
                 j = 2 * c + jj
-                h_t = psum.tile([P, 4, P], F32, tag="rot", name="h_t_%d" % j)
+                h_t = bank(j % 4, [P, 4, P], F32, "h_t_%d" % j)
                 for t in range(4):
                     nc.tensor.transpose(h_t[:, t, :], h_pre[j][:, t, :], ident_f[:])
                 nc.scalar.activation(
@@ -233,17 +250,9 @@ def tile_layernormmlp_w_kernel(
             h_words.append(words)
             h_plane.append(plane)
 
-        fc1(0)
-        for c in range(1, 4):
-            fc1(c)
-            finish_h(c - 1)
-        finish_h(3)
-
         acc2 = []
-        for j in range(4):
-            acc2_j = psum.tile([P, 512], F32, tag="fix", name="acc2_%d" % j)
-            acc2.append(acc2_j)
-        for g in range(8):
+
+        def fc2(g):
             for j in range(4):
                 if g < 7:
                     rhs = w2[g][:, 512 * j : 512 * (j + 1)]
@@ -258,6 +267,17 @@ def tile_layernormmlp_w_kernel(
                     start=(g == 0),
                     stop=(g == 7),
                 )
+
+        for c in range(3):
+            finish_h(c)
+        for j in range(4):
+            acc2_j = bank(4 + j, [P, 512], F32, "acc2_%d" % j)
+            acc2.append(acc2_j)
+        fc2(0)
+        fc2(1)
+        finish_h(3)
+        for g in range(2, 8):
+            fc2(g)
         for j in range(4):
             o_j = keep.tile([P, 512], F32, name="o_%d" % j)
             nc.vector.tensor_tensor(

@@ -62,28 +62,33 @@ def tile_layernormmlp_w_kernel(
         nc.sync.dma_start(out=vec_rows[4:8, :], in_=beta.rearrange("(c n) -> c n", n=512))
         nc.sync.dma_start(out=vec_rows[8:16, :], in_=fc1_bias.rearrange("(c n) -> c n", n=512))
         nc.sync.dma_start(out=vec_rows[16:20, :], in_=fc2_bias.rearrange("(c n) -> c n", n=512))
-        for q in range(4):
-            nc.gpsimd.dma_start(
-                out=planes1[32 * q : 32 * q + 16, :].bitcast(F32),
-                in_=fc1_kernel_scales[:, 4 * q : 4 * q + 4, :].bitcast(F32),
-            )
-        ident_f = keep.tile([P, P], F32)
-        make_identity(nc, ident_f[:])
-        for a in range(2):
+        def load_scales(plane, scales):
             for q in range(4):
                 nc.gpsimd.dma_start(
-                    out=planes2[32 * q : 32 * q + 16, a, :].bitcast(F32),
-                    in_=fc2_kernel_scales[4 * a : 4 * a + 4, 4 * q : 4 * q + 4, :].bitcast(F32),
+                    out=plane[32 * q : 32 * q + 16, :].bitcast(F32),
+                    in_=scales[:, 4 * q : 4 * q + 4, :].bitcast(F32),
                 )
+
         w1_view = fc1_kernel_words.rearrange("g p n t -> g p (n t)")
         w1 = []
+        ident_f = keep.tile([P, P], F32)
         for g in range(3):
             w1_g = keep.tile([P, F1], U32, name="w1_%d" % g, align_bytes=64)
+            if g == 1:
+                load_scales(planes1[:], fc1_kernel_scales)
+                make_identity(nc, ident_f[:])
+                nc.gpsimd.memset(w1_g[:, 0:8], 0)
+            if g == 2:
+                load_scales(planes2[:, 0, :], fc2_kernel_scales[0:4])
+                nc.gpsimd.memset(w1_g[:, 0:8], 0)
             nc.sync.dma_start(out=w1_g[:].bitcast(I32), in_=w1_view[g].bitcast(I32))
             w1.append(w1_g)
         w1_last = []
         for i in range(2):
             w1_l = keep.tile([P, F1 // 2], U32, name="w1_last_%d" % i, align_bytes=64)
+            if i == 0:
+                load_scales(planes2[:, 1, :], fc2_kernel_scales[4:8])
+                nc.gpsimd.memset(w1_l[:, 0:8], 0)
             nc.sync.dma_start(
                 out=w1_l[:].bitcast(I32), in_=w1_view[3][:, 8192 * i : 8192 * (i + 1)].bitcast(I32)
             )

@@ -74,11 +74,9 @@ def tile_layernormmlp_w_kernel(
         ident_f = keep.tile([P, P], F32)
         for g in range(3):
             w1_g = keep.tile([P, F1], U32, name="w1_%d" % g, align_bytes=64)
-            if g == 1:
+            if g == 2:
                 load_scales(planes1[:], fc1_kernel_scales)
                 make_identity(nc, ident_f[:])
-                nc.gpsimd.memset(w1_g[:, 0:8], 0)
-            if g == 2:
                 load_scales(planes2[:, 0, :], fc2_kernel_scales[0:4])
                 nc.gpsimd.memset(w1_g[:, 0:8], 0)
             nc.sync.dma_start(out=w1_g[:].bitcast(I32), in_=w1_view[g].bitcast(I32))
@@ -95,16 +93,17 @@ def tile_layernormmlp_w_kernel(
             w1_last.append(w1_l)
         w2_view = fc2_kernel_words.rearrange("g p n t -> g p (n t)")
         w2 = []
-        for g in range(7):
+        for g in range(6):
             w2_g = keep.tile([P, F2], U32, name="w2_%d" % g, align_bytes=64)
             nc.sync.dma_start(out=w2_g[:].bitcast(I32), in_=w2_view[g].bitcast(I32))
             w2.append(w2_g)
+        pieces = [(0, 512), (512, 1024), (1024, 1536), (1536, 1792), (1792, 2048)]
+        w2_pairs = fc2_kernel_words.rearrange("g p n t -> p g (n t)")
         w2_last = []
-        for j in range(4):
-            w2_l = keep.tile([P, 512], U32, name="w2_last_%d" % j, align_bytes=64)
+        for lo, hi in pieces:
+            w2_l = keep.tile([P, 2, hi - lo], U32, name="w2_last_%d" % lo, align_bytes=64)
             nc.sync.dma_start(
-                out=w2_l[:].bitcast(I32),
-                in_=w2_view[7][:, 2048 * j : 2048 * (j + 1)].bitcast(I32),
+                out=w2_l[:].bitcast(I32), in_=w2_pairs[:, 6:8, 4 * lo : 4 * hi].bitcast(I32)
             )
             w2_last.append(w2_l)
 
@@ -237,7 +236,7 @@ def tile_layernormmlp_w_kernel(
             grouped = work.tile([P, 2, P, 4], BF16, tag="h_grouped", name="h_grouped_%d" % c, align_bytes=64)
             for jj in range(2):
                 j = 2 * c + jj
-                h_t = bank(j % 4, [P, 4, P], F32, "h_t_%d" % j)
+                h_t = bank((0, 1, 2, 3, 0, 1, 0, 1)[j], [P, 4, P], F32, "h_t_%d" % j)
                 for t in range(4):
                     nc.tensor.transpose(h_t[:, t, :], h_pre[j][:, t, :], ident_f[:])
                 nc.scalar.activation(
@@ -257,35 +256,35 @@ def tile_layernormmlp_w_kernel(
 
         acc2 = []
 
-        def fc2(g):
-            for j in range(4):
-                if g < 7:
-                    rhs = w2[g][:, 512 * j : 512 * (j + 1)]
-                else:
-                    rhs = w2_last[j][:]
-                nc.tensor.matmul_mx(
-                    out=acc2[j][:],
-                    lhsT=h_words[g // 2][:, g % 2, :].bitcast(FP8X4),
-                    lhsT_scale=h_plane[g // 2][:, g % 2, :],
-                    rhs=rhs.bitcast(FP8X4),
-                    rhs_scale=planes2[4 * (g % 4) : P, g // 4, 512 * j : 512 * (j + 1)],
-                    start=(g == 0),
-                    stop=(g == 7),
-                )
+        def fc2(g, i):
+            lo, hi = pieces[i]
+            if g < 6:
+                rhs = w2[g][:, lo:hi]
+            else:
+                rhs = w2_last[i][:, g - 6, :]
+            nc.tensor.matmul_mx(
+                out=acc2[i][:],
+                lhsT=h_words[g // 2][:, g % 2, :].bitcast(FP8X4),
+                lhsT_scale=h_plane[g // 2][:, g % 2, :],
+                rhs=rhs.bitcast(FP8X4),
+                rhs_scale=planes2[4 * (g % 4) : P, g // 4, lo:hi],
+                start=(g == 0),
+                stop=(g == 7),
+            )
 
         for c in range(3):
             finish_h(c)
-        for j in range(4):
-            acc2_j = bank(4 + j, [P, 512], F32, "acc2_%d" % j)
-            acc2.append(acc2_j)
-        fc2(0)
-        fc2(1)
-        finish_h(3)
-        for g in range(2, 8):
-            fc2(g)
-        for j in range(4):
-            o_j = keep.tile([P, 512], F32, name="o_%d" % j)
-            nc.vector.tensor_tensor(
-                out=o_j[:], in0=acc2[j][:], in1=b2_all[:, 512 * j : 512 * (j + 1)], op=ALU.add
-            )
-            nc.sync.dma_start(out=out[:, 512 * j : 512 * (j + 1)], in_=o_j[:])
+        for i, (lo, hi) in enumerate(pieces):
+            acc2_i = bank((4, 5, 6, 7, 3)[i], [P, hi - lo], F32, "acc2_%d" % i)
+            acc2.append(acc2_i)
+        for g in range(6):
+            if g == 2:
+                finish_h(3)
+            for i in range(len(pieces)):
+                fc2(g, i)
+        for i, (lo, hi) in enumerate(pieces):
+            fc2(6, i)
+            fc2(7, i)
+            o_i = keep.tile([P, hi - lo], F32, name="o_%d" % i)
+            nc.vector.tensor_tensor(out=o_i[:], in0=acc2[i][:], in1=b2_all[:, lo:hi], op=ALU.add)
+            nc.sync.dma_start(out=out[:, lo:hi], in_=o_i[:])

@@ -116,33 +116,6 @@ def tile_layernormmlp_w_kernel(
                 stop=True,
             )
 
-        b2_all = keep.tile([P, F2], BF16)
-        for i in range(2):
-            b2_i = bank(4 + i, [P, 1024], BF16, "b2_bank_%d" % i)
-            spread(16 + 2 * i, b2_i, 0)
-            spread(16 + 2 * i + 1, b2_i, 1)
-            nc.scalar.copy(out=b2_all[:, 1024 * i : 1024 * (i + 1)], in_=b2_i[:])
-        gam = []
-        bet = []
-        for i in range(2):
-            gam_i = bank(i, [P, 1024], BF16, "gam_%d" % i)
-            spread(2 * i, gam_i, 0)
-            spread(2 * i + 1, gam_i, 1)
-            gam.append(gam_i)
-        for i in range(2):
-            bet_i = bank(2 + i, [P, 1024], BF16, "bet_%d" % i)
-            spread(4 + 2 * i, bet_i, 0)
-            spread(4 + 2 * i + 1, bet_i, 1)
-            bet.append(bet_i)
-        b1_sorted = []
-        for i in range(4):
-            b1_bank = bank((6, 7, 4, 5)[i], [P, 1024], BF16, "b1_bank_%d" % i)
-            spread(8 + 2 * i, b1_bank, 0)
-            spread(8 + 2 * i + 1, b1_bank, 1)
-            b1_i = keep.tile([P, 2, 4, P], BF16, name="b1_sorted_%d" % i)
-            nc.scalar.copy(out=b1_i[:], in_=b1_bank[:].rearrange("q (j p t) -> q j t p", j=2, t=4))
-            b1_sorted.append(b1_i)
-
         stats = keep.tile([P, 4, 6], F32)
         for i in range(4):
             nc.vector.bn_stats(out=stats[:, i, :], in_=x_sb[:, 512 * i : 512 * (i + 1)])
@@ -155,49 +128,96 @@ def tile_layernormmlp_w_kernel(
         std = keep.tile([P, 1], F32)
         nc.scalar.activation(out=std[:], in_=var_eps[:], func=ACT.Sqrt)
 
-        centred = keep.tile([P, D], F32)
+        gam = []
+        bet = []
         for i in range(2):
+            gam_i = bank(i, [P, 1024], BF16, "gam_%d" % i)
+            spread(2 * i, gam_i, 0)
+            spread(2 * i + 1, gam_i, 1)
+            gam.append(gam_i)
+            bet_i = bank(2 + i, [P, 1024], BF16, "bet_%d" % i)
+            spread(4 + 2 * i, bet_i, 0)
+            spread(4 + 2 * i + 1, bet_i, 1)
+            bet.append(bet_i)
+
+        b1_sorted = []
+
+        def load_b1(i):
+            b1_bank = bank(4 + i, [P, 1024], BF16, "b1_bank_%d" % i)
+            spread(8 + 2 * i, b1_bank, 0)
+            spread(8 + 2 * i + 1, b1_bank, 1)
+            b1_i = keep.tile([P, 2, 4, P], BF16, name="b1_sorted_%d" % i)
+            nc.scalar.copy(out=b1_i[:], in_=b1_bank[:].rearrange("q (j p t) -> q j t p", j=2, t=4))
+            b1_sorted.append(b1_i)
+
+        rstd = keep.tile([P, 1], F32)
+        ln_bf = keep.tile([P, D], BF16)
+
+        def normalise(i):
             cols = slice(1024 * i, 1024 * (i + 1))
+            centred = keep.tile([P, 1024], F32, name="centred_%d" % i)
             nc.vector.scalar_tensor_tensor(
-                out=centred[:, cols],
+                out=centred[:],
                 in0=x_sb[:, cols],
                 scalar=mean_var[:, 0:1],
                 in1=gam[i][:],
                 op0=ALU.subtract,
                 op1=ALU.mult,
             )
-        rstd = keep.tile([P, 1], F32)
-        nc.vector.reciprocal(out=rstd[:], in_=std[:])
-        ln_sorted = keep.tile([P, 4, 4, P], F32)
-        for g in range(4):
+            if i == 0:
+                nc.vector.reciprocal(out=rstd[:], in_=std[:])
             nc.vector.scalar_tensor_tensor(
-                out=ln_sorted[:, g],
-                in0=centred[:, 512 * g : 512 * (g + 1)].rearrange("q (p t) -> q t p", t=4),
+                out=ln_bf[:, cols],
+                in0=centred[:],
                 scalar=rstd[:, 0:1],
-                in1=bet[g // 2][:, 512 * (g % 2) : 512 * (g % 2 + 1)].rearrange(
-                    "q (p t) -> q t p", t=4
-                ),
+                in1=bet[i][:],
                 op0=ALU.mult,
                 op1=ALU.add,
             )
 
-        ln_grouped = keep.tile([P, 4, P, 4], BF16, align_bytes=64)
-        for g in range(4):
-            ln_t = bank(g, [P, 4, P], F32, "ln_t_%d" % g)
-            for t in range(4):
-                nc.tensor.transpose(ln_t[:, t, :], ln_sorted[:, g, t, :], ident_f[:])
-            if g % 2 == 0:
-                nc.scalar.copy(out=ln_grouped[:, g], in_=ln_t[:].rearrange("p t r -> p r t"))
-            else:
-                nc.vector.tensor_copy(out=ln_grouped[:, g], in_=ln_t[:].rearrange("p t r -> p r t"))
-        ln_words = keep.tile([P, 4, P], U32, align_bytes=64)
-        ln_plane = keep.tile([P, 4, P], U8, align_bytes=64)
-        nc.vector.quantize_mx(
-            out=ln_words[:].rearrange("p g m -> p (g m)").bitcast(FP8X4),
-            scales=ln_plane[:].rearrange("p g m -> p (g m)"),
-            in_=ln_grouped[:].rearrange("p g r t -> p (g r t)"),
-        )
+        ln_grouped = []
+        ln_words = []
+        ln_plane = []
+
+        def turn(i):
+            ln_t = bank(i, [P, 2, 2, P], F32, "ln_t_%d" % i)
+            words = ln_bf[:].bitcast(F32)
+            for gg in range(2):
+                g = 2 * i + gg
+                for u in range(2):
+                    nc.tensor.transpose(
+                        ln_t[:, gg, u, :], words[:, 256 * g + u : 256 * (g + 1) : 2], ident_f[:]
+                    )
+            grouped = keep.tile([P, 2, P, 4], BF16, name="ln_grouped_%d" % i, align_bytes=64)
+            copy = nc.scalar.copy if i == 0 else nc.vector.tensor_copy
+            copy(
+                out=grouped[:].bitcast(F32),
+                in_=ln_t[:].rearrange("p g u r -> p g r u"),
+            )
+            ln_grouped.append(grouped)
+
+        def quantise_ln(i):
+            words = keep.tile([P, 2, P], U32, name="ln_words_%d" % i, align_bytes=64)
+            plane = keep.tile([P, 2, P], U8, name="ln_plane_%d" % i, align_bytes=64)
+            nc.vector.quantize_mx(
+                out=words[:].rearrange("p g m -> p (g m)").bitcast(FP8X4),
+                scales=plane[:].rearrange("p g m -> p (g m)"),
+                in_=ln_grouped[i][:].rearrange("p g r t -> p (g r t)"),
+            )
+            ln_words.append(words)
+            ln_plane.append(plane)
+
+        normalise(0)
+        load_b1(0)
+        load_b1(1)
+        turn(0)
         nc.scalar.activation(out=table_out[:, 1:2], in_=table[:], func=ACT.Gelu_apprx_tanh)
+        normalise(1)
+        quantise_ln(0)
+        load_b1(2)
+        load_b1(3)
+        turn(1)
+        quantise_ln(1)
 
         h_words = []
         h_plane = []
@@ -206,31 +226,34 @@ def tile_layernormmlp_w_kernel(
         for j in range(8):
             acc1_j = bank(j, [P, 512], F32, "acc1_%d" % j)
             acc1.append(acc1_j)
-        for g in range(4):
-            for j in range(8):
+
+        def fc1(g, columns):
+            for j in columns:
                 if g < 3:
                     rhs = w1[g][:, 512 * j : 512 * (j + 1)]
                 else:
                     rhs = w1_last[j // 4][:, 512 * (j % 4) : 512 * (j % 4 + 1)]
                 nc.tensor.matmul_mx(
                     out=acc1[j][:],
-                    lhsT=ln_words[:, g, :].bitcast(FP8X4),
-                    lhsT_scale=ln_plane[:, g, :],
+                    lhsT=ln_words[g // 2][:, g % 2, :].bitcast(FP8X4),
+                    lhsT_scale=ln_plane[g // 2][:, g % 2, :],
                     rhs=rhs.bitcast(FP8X4),
                     rhs_scale=planes1[4 * g : P, 512 * j : 512 * (j + 1)],
                     start=(g == 0),
                     stop=(g == 3),
                 )
         h_pre = []
-        for j in range(8):
-            pre = keep.tile([P, 4, P], F32, name="h_pre_%d" % j)
-            nc.vector.tensor_tensor(
-                out=pre[:],
-                in0=acc1[j][:].rearrange("q (p t) -> q t p", t=4),
-                in1=b1_sorted[j // 2][:, j % 2],
-                op=ALU.add,
-            )
-            h_pre.append(pre)
+
+        def add_b1(columns):
+            for j in columns:
+                pre = keep.tile([P, 4, P], F32, name="h_pre_%d" % j)
+                nc.vector.tensor_tensor(
+                    out=pre[:],
+                    in0=acc1[j][:].rearrange("q (p t) -> q t p", t=4),
+                    in1=b1_sorted[j // 2][:, j % 2],
+                    op=ALU.add,
+                )
+                h_pre.append(pre)
 
         def finish_h(c):
             grouped = work.tile([P, 2, P, 4], BF16, tag="h_grouped", name="h_grouped_%d" % c, align_bytes=64)
@@ -272,14 +295,28 @@ def tile_layernormmlp_w_kernel(
                 stop=(g == 7),
             )
 
-        for c in range(3):
-            finish_h(c)
+        for g in range(3):
+            fc1(g, (2, 3, 0, 1, 4, 5, 6, 7))
+        fc1(3, range(4))
+        add_b1(range(4))
+        finish_h(0)
+        fc1(3, range(4, 8))
+        add_b1(range(4, 8))
+        finish_h(1)
+        finish_h(2)
         for i, (lo, hi) in enumerate(pieces):
             acc2_i = bank((4, 5, 6, 7, 3)[i], [P, hi - lo], F32, "acc2_%d" % i)
             acc2.append(acc2_i)
+        b2_all = keep.tile([P, F2], BF16)
         for g in range(6):
             if g == 2:
                 finish_h(3)
+            if g == 4:
+                for i in range(2):
+                    b2_bank = bank((2, 0)[i], [P, 1024], BF16, "b2_bank_%d" % i)
+                    spread(16 + 2 * i, b2_bank, 0)
+                    spread(16 + 2 * i + 1, b2_bank, 1)
+                    nc.scalar.copy(out=b2_all[:, 1024 * i : 1024 * (i + 1)], in_=b2_bank[:])
             for i in range(len(pieces)):
                 fc2(g, i)
         for i, (lo, hi) in enumerate(pieces):

@@ -51,6 +51,8 @@ def tile_layernormmlp_w_kernel(
         nc.vector.memset(planes2[:].bitcast(I32), 0)
         ident_bf = keep.tile([P, P], BF16)
         make_identity(nc, ident_bf[:])
+        ident_f = keep.tile([P, P], F32)
+        make_identity(nc, ident_f[:])
         table = keep.tile([P, 1], F32)
         nc.vector.memset(table[:], 1.0)
         table_out = keep.tile([P, 2], F32)
@@ -71,12 +73,12 @@ def tile_layernormmlp_w_kernel(
 
         w1_view = fc1_kernel_words.rearrange("g p n t -> g p (n t)")
         w1 = []
-        ident_f = keep.tile([P, P], F32)
         for g in range(3):
             w1_g = keep.tile([P, F1], U32, name="w1_%d" % g, align_bytes=64)
-            if g == 2:
+            if g == 1:
                 load_scales(planes1[:], fc1_kernel_scales)
-                make_identity(nc, ident_f[:])
+                nc.gpsimd.memset(w1_g[:, 0:8], 0)
+            if g == 2:
                 load_scales(planes2[:, 0, :], fc2_kernel_scales[0:4])
                 nc.gpsimd.memset(w1_g[:, 0:8], 0)
             nc.sync.dma_start(out=w1_g[:].bitcast(I32), in_=w1_view[g].bitcast(I32))

@@ -44,7 +44,7 @@ def tile_layernormmlp_w_kernel(
             return psum.tile(shape, dtype, tag="bank%d" % i, name=name)
 
         vec_rows = keep.tile([P, 512], BF16)
-        nc.vector.memset(vec_rows[:].bitcast(I32), 0)
+        nc.gpsimd.memset(vec_rows[:].bitcast(I32), 0)
         planes1 = keep.tile([P, F1], U8, align_bytes=64)
         nc.vector.memset(planes1[:].bitcast(I32), 0)
         planes2 = keep.tile([P, 2, F2], U8, align_bytes=64)
@@ -100,14 +100,23 @@ def tile_layernormmlp_w_kernel(
             nc.sync.dma_start(out=w2_g[:].bitcast(I32), in_=w2_view[g].bitcast(I32))
             w2.append(w2_g)
         pieces = [(0, 512), (512, 1024), (1024, 1536), (1536, 1792), (1792, 2048)]
-        w2_pairs = fc2_kernel_words.rearrange("g p n t -> p g (n t)")
-        w2_last = []
-        for lo, hi in pieces:
-            w2_l = keep.tile([P, 2, hi - lo], U32, name="w2_last_%d" % lo, align_bytes=64)
+        w2_last = {}
+        for g, lo, hi in (
+            (6, 0, 1024),
+            (7, 0, 1024),
+            (6, 1024, 1536),
+            (7, 1024, 1536),
+            (6, 1536, 2048),
+            (7, 1536, 1792),
+            (7, 1792, 2048),
+        ):
+            w2_l = keep.tile([P, hi - lo], U32, name="w2_last_%d_%d" % (g, lo), align_bytes=64)
             nc.sync.dma_start(
-                out=w2_l[:].bitcast(I32), in_=w2_pairs[:, 6:8, 4 * lo : 4 * hi].bitcast(I32)
+                out=w2_l[:].bitcast(I32), in_=w2_view[g][:, 4 * lo : 4 * hi].bitcast(I32)
             )
-            w2_last.append(w2_l)
+            for piece in pieces:
+                if lo <= piece[0] and piece[1] <= hi:
+                    w2_last[g, piece] = w2_l[:, piece[0] - lo : piece[1] - lo]
 
         def spread(row, dest, half):
             nc.tensor.matmul(
@@ -286,7 +295,7 @@ def tile_layernormmlp_w_kernel(
             if g < 6:
                 rhs = w2[g][:, lo:hi]
             else:
-                rhs = w2_last[i][:, g - 6, :]
+                rhs = w2_last[g, pieces[i]]
             nc.tensor.matmul_mx(
                 out=acc2[i][:],
                 lhsT=h_words[g // 2][:, g % 2, :].bitcast(FP8X4),
@@ -321,9 +330,14 @@ def tile_layernormmlp_w_kernel(
                     nc.scalar.copy(out=b2_all[:, 1024 * i : 1024 * (i + 1)], in_=b2_bank[:])
             for i in range(len(pieces)):
                 fc2(g, i)
-        for i, (lo, hi) in enumerate(pieces):
-            fc2(6, i)
-            fc2(7, i)
-            o_i = keep.tile([P, hi - lo], F32, name="o_%d" % i)
-            nc.vector.tensor_tensor(out=o_i[:], in0=acc2[i][:], in1=b2_all[:, lo:hi], op=ALU.add)
-            nc.sync.dma_start(out=out[:, lo:hi], in_=o_i[:])
+        for together in ((0, 1), (2,), (3, 4)):
+            for i in together:
+                fc2(6, i)
+            for i in together:
+                fc2(7, i)
+                lo, hi = pieces[i]
+                o_i = keep.tile([P, hi - lo], F32, name="o_%d" % i)
+                nc.vector.tensor_tensor(
+                    out=o_i[:], in0=acc2[i][:], in1=b2_all[:, lo:hi], op=ALU.add
+                )
+                nc.sync.dma_start(out=out[:, lo:hi], in_=o_i[:])

from contextlib import ExitStack

import concourse.mybir as mybir
from concourse.masks import make_identity

F32 = mybir.dt.float32
BF16 = mybir.dt.bfloat16
I32 = mybir.dt.int32
U32 = mybir.dt.uint32
U8 = mybir.dt.uint8
FP8X4 = mybir.dt.float8_e4m3fn_x4
ALU = mybir.AluOpType
ACT = mybir.ActivationFunctionType

P = 128
D = 2048
F1 = 4096
F2 = 2048
EPS = 1e-3
FLOPS = 2 * P * (D * F1 + F1 * F2)


def tile_layernormmlp_w_kernel(
    tc,
    inputs,
    gamma,
    beta,
    fc1_kernel_words,
    fc1_kernel_scales,
    fc1_bias,
    fc2_kernel_words,
    fc2_kernel_scales,
    fc2_bias,
    out,
):
    nc = tc.nc
    with ExitStack() as ctx:
        keep = ctx.enter_context(tc.tile_pool(name="keep", bufs=1))
        work = ctx.enter_context(tc.tile_pool(name="work", bufs=4))
        psum = ctx.enter_context(tc.psum_pool(name="psum", bufs=1))
        ctx.enter_context(tc.manual_schedule())

        def bank(i, shape, dtype, name):
            return psum.tile(shape, dtype, tag="bank%d" % i, name=name)

        vec_rows = keep.tile([P, 512], BF16)
        nc.gpsimd.memset(vec_rows[:].bitcast(I32), 0)
        planes1 = keep.tile([P, F1], U8, align_bytes=64)
        nc.vector.memset(planes1[:].bitcast(I32), 0)
        planes2 = keep.tile([P, 2, F2], U8, align_bytes=64)
        nc.vector.memset(planes2[:].bitcast(I32), 0)
        ident_bf = keep.tile([P, P], BF16)
        make_identity(nc, ident_bf[:])
        ident_f = keep.tile([P, P], F32)
        make_identity(nc, ident_f[:])
        table = keep.tile([P, 1], F32)
        nc.vector.memset(table[:], 1.0)
        table_out = keep.tile([P, 2], F32)
        nc.scalar.activation(out=table_out[:, 0:1], in_=table[:], func=ACT.Sqrt)

        x_sb = keep.tile([P, D], BF16)
        nc.sync.dma_start(out=x_sb[:], in_=inputs)
        nc.sync.dma_start(out=vec_rows[0:4, :], in_=gamma.rearrange("(c n) -> c n", n=512))
        nc.sync.dma_start(out=vec_rows[4:8, :], in_=beta.rearrange("(c n) -> c n", n=512))
        nc.sync.dma_start(out=vec_rows[8:16, :], in_=fc1_bias.rearrange("(c n) -> c n", n=512))
        nc.sync.dma_start(out=vec_rows[16:20, :], in_=fc2_bias.rearrange("(c n) -> c n", n=512))
        def load_scales(plane, scales):
            for q in range(4):
                nc.gpsimd.dma_start(
                    out=plane[32 * q : 32 * q + 16, :].bitcast(F32),
                    in_=scales[:, 4 * q : 4 * q + 4, :].bitcast(F32),
                )

        w1_view = fc1_kernel_words.rearrange("g p n t -> g p (n t)")
        w1 = []
        for g in range(3):
            w1_g = keep.tile([P, F1], U32, name="w1_%d" % g, align_bytes=64)
            if g == 1:
                load_scales(planes1[:], fc1_kernel_scales)
                nc.gpsimd.memset(w1_g[:, 0:8], 0)
            if g == 2:
                load_scales(planes2[:, 0, :], fc2_kernel_scales[0:4])
                nc.gpsimd.memset(w1_g[:, 0:8], 0)
            nc.sync.dma_start(out=w1_g[:].bitcast(I32), in_=w1_view[g].bitcast(I32))
            w1.append(w1_g)
        w1_last = []
        for i in range(2):
            w1_l = keep.tile([P, F1 // 2], U32, name="w1_last_%d" % i, align_bytes=64)
            if i == 0:
                load_scales(planes2[:, 1, :], fc2_kernel_scales[4:8])
                nc.gpsimd.memset(w1_l[:, 0:8], 0)
            nc.sync.dma_start(
                out=w1_l[:].bitcast(I32), in_=w1_view[3][:, 8192 * i : 8192 * (i + 1)].bitcast(I32)
            )
            w1_last.append(w1_l)
        w2_view = fc2_kernel_words.rearrange("g p n t -> g p (n t)")
        w2 = []
        for g in range(6):
            w2_g = keep.tile([P, F2], U32, name="w2_%d" % g, align_bytes=64)
            nc.sync.dma_start(out=w2_g[:].bitcast(I32), in_=w2_view[g].bitcast(I32))
            w2.append(w2_g)
        pieces = [(0, 512), (512, 1024), (1024, 1536), (1536, 1792), (1792, 2048)]
        w2_last = {}
        for g, lo, hi in (
            (6, 0, 1024),
            (7, 0, 1024),
            (6, 1024, 1536),
            (7, 1024, 1536),
            (6, 1536, 2048),
            (7, 1536, 1792),
            (7, 1792, 2048),
        ):
            w2_l = keep.tile([P, hi - lo], U32, name="w2_last_%d_%d" % (g, lo), align_bytes=64)
            nc.sync.dma_start(
                out=w2_l[:].bitcast(I32), in_=w2_view[g][:, 4 * lo : 4 * hi].bitcast(I32)
            )
            for piece in pieces:
                if lo <= piece[0] and piece[1] <= hi:
                    w2_last[g, piece] = w2_l[:, piece[0] - lo : piece[1] - lo]

        def spread(row, dest, half):
            nc.tensor.matmul(
                out=dest[:, 512 * half : 512 * (half + 1)],
                lhsT=ident_bf[:, row : row + 1].to_broadcast([P, P]),
                rhs=vec_rows[:],
                start=True,
                stop=True,
            )

        stats = keep.tile([P, 4, 6], F32)
        for i in range(4):
            nc.vector.bn_stats(out=stats[:, i, :], in_=x_sb[:, 512 * i : 512 * (i + 1)])
        mean_var = keep.tile([P, 2], F32)
        nc.vector.bn_aggr(out=mean_var[:], in_=stats[:].rearrange("p a b -> p (a b)"))
        var_eps = keep.tile([P, 1], F32)
        nc.vector.tensor_scalar(
            out=var_eps[:], in0=mean_var[:, 1:2], scalar1=EPS, scalar2=None, op0=ALU.add
        )
        std = keep.tile([P, 1], F32)
        nc.scalar.activation(out=std[:], in_=var_eps[:], func=ACT.Sqrt)

        gam = []
        bet = []
        for i in range(2):
            gam_i = bank(i, [P, 1024], BF16, "gam_%d" % i)
            spread(2 * i, gam_i, 0)
            spread(2 * i + 1, gam_i, 1)
            gam.append(gam_i)
            bet_i = bank(2 + i, [P, 1024], BF16, "bet_%d" % i)
            spread(4 + 2 * i, bet_i, 0)
            spread(4 + 2 * i + 1, bet_i, 1)
            bet.append(bet_i)

        b1_sorted = []

        def load_b1(i):
            b1_bank = bank(4 + i, [P, 1024], BF16, "b1_bank_%d" % i)
            spread(8 + 2 * i, b1_bank, 0)
            spread(8 + 2 * i + 1, b1_bank, 1)
            b1_i = keep.tile([P, 2, 4, P], BF16, name="b1_sorted_%d" % i)
            nc.scalar.copy(out=b1_i[:], in_=b1_bank[:].rearrange("q (j p t) -> q j t p", j=2, t=4))
            b1_sorted.append(b1_i)

        rstd = keep.tile([P, 1], F32)
        ln_bf = keep.tile([P, D], BF16)

        def normalise(i):
            cols = slice(1024 * i, 1024 * (i + 1))
            centred = keep.tile([P, 1024], F32, name="centred_%d" % i)
            nc.vector.scalar_tensor_tensor(
                out=centred[:],
                in0=x_sb[:, cols],
                scalar=mean_var[:, 0:1],
                in1=gam[i][:],
                op0=ALU.subtract,
                op1=ALU.mult,
            )
            if i == 0:
                nc.vector.reciprocal(out=rstd[:], in_=std[:])
            nc.vector.scalar_tensor_tensor(
                out=ln_bf[:, cols],
                in0=centred[:],
                scalar=rstd[:, 0:1],
                in1=bet[i][:],
                op0=ALU.mult,
                op1=ALU.add,
            )

        ln_grouped = []
        ln_words = []
        ln_plane = []

        def turn(i):
            ln_t = bank(i, [P, 2, 2, P], F32, "ln_t_%d" % i)
            words = ln_bf[:].bitcast(F32)
            for gg in range(2):
                g = 2 * i + gg
                for u in range(2):
                    nc.tensor.transpose(
                        ln_t[:, gg, u, :], words[:, 256 * g + u : 256 * (g + 1) : 2], ident_f[:]
                    )
            grouped = keep.tile([P, 2, P, 4], BF16, name="ln_grouped_%d" % i, align_bytes=64)
            copy = nc.scalar.copy if i == 0 else nc.vector.tensor_copy
            copy(
                out=grouped[:].bitcast(F32),
                in_=ln_t[:].rearrange("p g u r -> p g r u"),
            )
            ln_grouped.append(grouped)

        def quantise_ln(i):
            words = keep.tile([P, 2, P], U32, name="ln_words_%d" % i, align_bytes=64)
            plane = keep.tile([P, 2, P], U8, name="ln_plane_%d" % i, align_bytes=64)
            nc.vector.quantize_mx(
                out=words[:].rearrange("p g m -> p (g m)").bitcast(FP8X4),
                scales=plane[:].rearrange("p g m -> p (g m)"),
                in_=ln_grouped[i][:].rearrange("p g r t -> p (g r t)"),
            )
            ln_words.append(words)
            ln_plane.append(plane)

        normalise(0)
        load_b1(0)
        load_b1(1)
        turn(0)
        nc.scalar.activation(out=table_out[:, 1:2], in_=table[:], func=ACT.Gelu_apprx_tanh)
        normalise(1)
        quantise_ln(0)
        load_b1(2)
        load_b1(3)
        turn(1)
        quantise_ln(1)

        h_words = []
        h_plane = []

        acc1 = []
        for j in range(8):
            acc1_j = bank(j, [P, 512], F32, "acc1_%d" % j)
            acc1.append(acc1_j)

        def fc1(g, columns):
            for j in columns:
                if g < 3:
                    rhs = w1[g][:, 512 * j : 512 * (j + 1)]
                else:
                    rhs = w1_last[j // 4][:, 512 * (j % 4) : 512 * (j % 4 + 1)]
                nc.tensor.matmul_mx(
                    out=acc1[j][:],
                    lhsT=ln_words[g // 2][:, g % 2, :].bitcast(FP8X4),
                    lhsT_scale=ln_plane[g // 2][:, g % 2, :],
                    rhs=rhs.bitcast(FP8X4),
                    rhs_scale=planes1[4 * g : P, 512 * j : 512 * (j + 1)],
                    start=(g == 0),
                    stop=(g == 3),
                )
        h_pre = []

        def add_b1(columns):
            for j in columns:
                pre = keep.tile([P, 4, P], F32, name="h_pre_%d" % j)
                nc.vector.tensor_tensor(
                    out=pre[:],
                    in0=acc1[j][:].rearrange("q (p t) -> q t p", t=4),
                    in1=b1_sorted[j // 2][:, j % 2],
                    op=ALU.add,
                )
                h_pre.append(pre)

        def finish_h(c):
            grouped = work.tile([P, 2, P, 4], BF16, tag="h_grouped", name="h_grouped_%d" % c, align_bytes=64)
            for jj in range(2):
                j = 2 * c + jj
                h_t = bank((0, 1, 2, 3, 0, 1, 0, 1)[j], [P, 4, P], F32, "h_t_%d" % j)
                for t in range(4):
                    nc.tensor.transpose(h_t[:, t, :], h_pre[j][:, t, :], ident_f[:])
                nc.scalar.activation(
                    out=grouped[:, jj],
                    in_=h_t[:].rearrange("p t r -> p r t"),
                    func=ACT.Gelu_apprx_tanh,
                )
            words = keep.tile([P, 2, P], U32, name="h_words_%d" % c, align_bytes=64)
            plane = keep.tile([P, 2, P], U8, name="h_plane_%d" % c, align_bytes=64)
            nc.vector.quantize_mx(
                out=words[:].rearrange("p j m -> p (j m)").bitcast(FP8X4),
                scales=plane[:].rearrange("p j m -> p (j m)"),
                in_=grouped[:].rearrange("p j r t -> p (j r t)"),
            )
            h_words.append(words)
            h_plane.append(plane)

        acc2 = []

        def fc2(g, i):
            lo, hi = pieces[i]
            if g < 6:
                rhs = w2[g][:, lo:hi]
            else:
                rhs = w2_last[g, pieces[i]]
            nc.tensor.matmul_mx(
                out=acc2[i][:],
                lhsT=h_words[g // 2][:, g % 2, :].bitcast(FP8X4),
                lhsT_scale=h_plane[g // 2][:, g % 2, :],
                rhs=rhs.bitcast(FP8X4),
                rhs_scale=planes2[4 * (g % 4) : P, g // 4, lo:hi],
                start=(g == 0),
                stop=(g == 7),
            )

        for g in range(3):
            fc1(g, (2, 3, 0, 1, 4, 5, 6, 7))
        fc1(3, range(4))
        add_b1(range(4))
        finish_h(0)
        fc1(3, range(4, 8))
        add_b1(range(4, 8))
        finish_h(1)
        finish_h(2)
        for i, (lo, hi) in enumerate(pieces):
            acc2_i = bank((4, 5, 6, 7, 3)[i], [P, hi - lo], F32, "acc2_%d" % i)
            acc2.append(acc2_i)
        b2_all = keep.tile([P, F2], BF16)
        for g in range(6):
            if g == 2:
                finish_h(3)
            if g == 4:
                for i in range(2):
                    b2_bank = bank((2, 0)[i], [P, 1024], BF16, "b2_bank_%d" % i)
                    spread(16 + 2 * i, b2_bank, 0)
                    spread(16 + 2 * i + 1, b2_bank, 1)
                    nc.scalar.copy(out=b2_all[:, 1024 * i : 1024 * (i + 1)], in_=b2_bank[:])
            for i in range(len(pieces)):
                fc2(g, i)
        for together in ((0, 1), (2,), (3, 4)):
            for i in together:
                fc2(6, i)
            for i in together:
                fc2(7, i)
                lo, hi = pieces[i]
                o_i = keep.tile([P, hi - lo], F32, name="o_%d" % i)
                nc.vector.tensor_tensor(
                    out=o_i[:], in0=acc2[i][:], in1=b2_all[:, lo:hi], op=ALU.add
                )
                nc.sync.dma_start(out=out[:, lo:hi], in_=o_i[:])
